import numpy as np
import ml_dtypes


def mxq(x, axis, fmt="e4m3"):
    dtype, down = {"e4m3": (ml_dtypes.float8_e4m3fn, 7), "e5m2": (ml_dtypes.float8_e5m2, 14)}[fmt]
    v = np.moveaxis(np.asarray(x, np.float32).astype(ml_dtypes.bfloat16).astype(np.float64), axis, -1)
    blocks = v.reshape(v.shape[:-1] + (-1, 32))
    amax = np.abs(blocks).max(-1, keepdims=True)
    byte = np.maximum(np.where(amax > 0, np.frexp(amax)[1] - 1 + 127, 0) - down, 1)
    scale = np.exp2(byte - 127.0)
    codes = (blocks / scale).astype(np.float32).astype(dtype).astype(np.float64)
    return np.moveaxis((codes * scale).reshape(v.shape), -1, axis)


WIDE = False


def mx_kscale(k):
    if not WIDE:
        return np.ones(k)
    levels = np.array([30, -30])
    if k % 512:
        return np.exp2(np.random.permutation(np.resize(levels, k // 32))).repeat(32)
    a = np.empty((k // 512, 16))
    for p in range(k // 512):
        a[p, :8] = np.random.permutation(np.resize(levels, 8))
        for g in range(8):
            far = levels[np.abs(levels - a[p, g]) >= 10]
            a[p, g + 8] = far[np.random.randint(len(far))]
    return np.exp2(a.ravel()).repeat(32)


BF16 = ml_dtypes.bfloat16


def bf(x):
    return np.asarray(x, np.float32).astype(BF16)


def f64(x):
    return np.asarray(x).astype(np.float64)


B, S, HID, H, KV, D, WIN, QB, KSZ = 1, 2048, 1024, 8, 2, 128, 384, 128, 4
EPS = 1e-5
QD, KVD = H * D, KV * D
C = QD + 2 * KVD


def silu(v):
    return v / (1.0 + np.exp(-v))


def rmsnorm(v, w):
    return v * (1.0 / np.sqrt(np.mean(v * v, axis=-1, keepdims=True) + EPS)) * w


def rotate_half(v):
    h = v.shape[-1] // 2
    return np.concatenate([-v[..., h:], v[..., :h]], axis=-1)


def canon(v, w, b):
    vp = np.pad(v, ((0, 0), (KSZ - 1, 0), (0, 0)))
    y = sum(vp[:, k:k + S, :] * w[:, k] for k in range(KSZ))
    return silu(y + b) + v


def setup_inputs():
    s = mx_kscale(HID)
    sd = 1.0 / np.sqrt(HID)
    inv_freq = 1.0 / (1e6 ** (np.arange(0, D, 2) / D))
    emb = np.concatenate([np.arange(S)[:, None] * inv_freq[None, :]] * 2, axis=-1)
    return {"x": bf(np.random.standard_normal((B, S, HID)) * s),
            "cos": bf(np.cos(emb)), "sin": bf(np.sin(emb)),
            "q_w": bf(np.random.standard_normal((QD, HID)) * sd / s[None, :]),
            "k_w": bf(np.random.standard_normal((KVD, HID)) * sd / s[None, :]),
            "v_w": bf(np.random.standard_normal((KVD, HID)) * sd / s[None, :]),
            "q_norm_w": bf(1.0 + 0.1 * np.random.standard_normal(D)),
            "k_norm_w": bf(1.0 + 0.1 * np.random.standard_normal(D)),
            "canon_w": bf(np.random.standard_normal((C, KSZ)) * 0.5),
            "canon_bias": bf(np.random.standard_normal(C) * 0.3)}


def reference(x, cos, sin, q_w, k_w, v_w, q_norm_w, k_norm_w, canon_w, canon_bias):
    xm = mxq(f64(x), 2, "e5m2")
    q = (xm @ mxq(f64(q_w), 1, "e4m3").T).reshape(B, S, H, D)
    k = (xm @ mxq(f64(k_w), 1, "e4m3").T).reshape(B, S, KV, D)
    v = xm @ mxq(f64(v_w), 1, "e4m3").T
    q = rmsnorm(q, f64(q_norm_w))
    k = rmsnorm(k, f64(k_norm_w))
    u = np.concatenate([q.reshape(B, S, QD), k.reshape(B, S, KVD), v], axis=-1)
    z = canon(u, f64(canon_w), f64(canon_bias))
    q = z[..., :QD].reshape(B, S, H, D)
    k = z[..., QD:QD + KVD].reshape(B, S, KV, D)
    v = z[..., QD + KVD:].reshape(B, S, KV, D)
    c, sn = f64(cos)[:, None, :], f64(sin)[:, None, :]
    return q * c + rotate_half(q) * sn, k * c + rotate_half(k) * sn, v

@@ -1,0 +1,415 @@
+from contextlib import ExitStack
+
+import concourse.mybir as mybir
+from concourse.masks import make_identity
+
+S, HID, D = 2048, 1024, 128
+Q_HEADS, KV_HEADS = 8, 2
+HEADS = Q_HEADS + 2 * KV_HEADS
+TAPS = 4
+EPS = 1e-5
+FLOPS = 2 * S * HID * HEADS * D
+
+F32 = mybir.dt.float32
+BF16 = mybir.dt.bfloat16
+U32 = mybir.dt.uint32
+U8 = mybir.dt.uint8
+E4M3 = mybir.dt.float8_e4m3fn_x4
+E5M2 = mybir.dt.float8_e5m2_x4
+ALU = mybir.AluOpType
+ACT = mybir.ActivationFunctionType
+
+P = 128
+PASSES = HID // 512
+TILES = S // P
+BLOCK_TILES = 4
+BLOCK = BLOCK_TILES * P
+BLOCKS = S // BLOCK
+HALO = TAPS - 1
+ACC_W = 520
+STEPS = BLOCKS * HEADS
+LEAD = 7
+K0 = Q_HEADS
+V0 = Q_HEADS + KV_HEADS
+
+
+def tile_attention_pa_kernel(tc, x, cos, sin, q_w, k_w, v_w, q_norm_w, k_norm_w,
+                                         canon_w, canon_bias, out_0, out_1, out_2):
+    nc = tc.nc
+    with ExitStack() as ctx:
+        keep = ctx.enter_context(tc.tile_pool(name="keep", bufs=1))
+        work = ctx.enter_context(tc.tile_pool(name="work", bufs=1))
+        psum = ctx.enter_context(tc.psum_pool(name="psum", bufs=1))
+        ctx.enter_context(tc.manual_schedule())
+
+        def bank(tag):
+            return psum.tile([P, 512], F32, name=tag, tag=tag)
+
+        ident = keep.tile([P, P], F32)
+        make_identity(nc, ident[:])
+
+        x_rows = x.rearrange("b (i p) k -> p (b i) k", p=P)
+        q_rows = q_w.rearrange("(i p) k -> p i k", p=P)
+        w_raw = keep.tile([P, HEADS, HID], BF16)
+        x_raw = keep.tile([P, TILES, HID], BF16)
+        cos_sb = keep.tile([P, TILES, D], BF16)
+        sin_sb = keep.tile([P, TILES, D], BF16)
+        nc.sync.dma_start(out=w_raw[:, 0:2, :], in_=q_rows[:, 0:2, :])
+        nc.sync.dma_start(out=w_raw[:, 2:4, :], in_=q_rows[:, 2:4, :])
+        nc.sync.dma_start(out=x_raw[:, 0:2, :], in_=x_rows[:, 0:2, :])
+        nc.sync.dma_start(out=x_raw[:, 2:4, :], in_=x_rows[:, 2:4, :])
+        nc.sync.dma_start(out=w_raw[:, 4:8, :], in_=q_rows[:, 4:8, :])
+        nc.sync.dma_start(out=w_raw[:, K0:V0, :], in_=k_w.rearrange("(i p) k -> p i k", p=P))
+        nc.sync.dma_start(out=w_raw[:, V0:HEADS, :], in_=v_w.rearrange("(i p) k -> p i k", p=P))
+        nc.sync.dma_start(out=x_raw[:, 4:8, :], in_=x_rows[:, 4:8, :])
+        nc.sync.dma_start(out=cos_sb[:], in_=cos.rearrange("(i p) d -> p i d", p=P))
+        nc.sync.dma_start(out=sin_sb[:], in_=sin.rearrange("(i p) d -> p i d", p=P))
+        nc.sync.dma_start(out=x_raw[:, 8:12, :], in_=x_rows[:, 8:12, :])
+        nc.sync.dma_start(out=x_raw[:, 12:16, :], in_=x_rows[:, 12:16, :])
+
+        par_raw = keep.tile([P, (TAPS + 1) * D], BF16)
+        nc.gpsimd.memset(par_raw[:], 0.0)
+        nc.scalar.dma_start(out=par_raw[0:HEADS, 0:TAPS * D], in_=canon_w.rearrange("(h p) j -> h (p j)", p=P))
+        nc.scalar.dma_start(out=par_raw[0:HEADS, TAPS * D:], in_=canon_bias.rearrange("(h p) -> h p", p=P))
+        nc.scalar.dma_start(out=par_raw[HEADS:HEADS + 1, TAPS * D:], in_=q_norm_w.rearrange("(o d) -> o d", o=1))
+        nc.scalar.dma_start(out=par_raw[HEADS + 1:HEADS + 2, TAPS * D:], in_=k_norm_w.rearrange("(o d) -> o d", o=1))
+        par_rows = keep.tile([P, TAPS + 1, D], F32)
+        nc.gpsimd.tensor_copy(out=par_rows[:, 0:TAPS, :], in_=par_raw[:, 0:TAPS * D].rearrange("p (c j) -> p j c", j=TAPS))
+        nc.gpsimd.tensor_copy(out=par_rows[:, TAPS, :], in_=par_raw[:, TAPS * D:])
+        minus_half = keep.tile([P, 4], F32)
+        nc.gpsimd.memset(minus_half[:], -0.5)
+        par = keep.tile([P, TAPS + 1, 16], F32)
+        tap_n = keep.tile([P, TAPS - 1, V0], F32)
+
+        def constants(tag_a, tag_b):
+            a = bank(tag_a)
+            b = bank(tag_b)
+            for j in range(TAPS):
+                nc.tensor.transpose(a[:, j * D:(j + 1) * D], par_rows[:, j, :], ident[:])
+            nc.tensor.transpose(b[:, 0:D], par_rows[:, TAPS, :], ident[:])
+            nc.vector.tensor_copy(out=par[:, 0:TAPS, :], in_=a[:].rearrange("p (j c) -> p j c", j=TAPS)[:, :, 0:16])
+            nc.vector.tensor_copy(out=par[:, TAPS, :], in_=b[:, 0:16])
+
+        def fold_norm_weights():
+            nc.vector.tensor_scalar(out=tap_n[:, :, 0:K0], in0=par[:, 1:TAPS, 0:K0],
+                                    scalar1=par[:, TAPS, HEADS:HEADS + 1], scalar2=None, op0=ALU.mult)
+            nc.vector.tensor_scalar(out=tap_n[:, :, K0:V0], in0=par[:, 1:TAPS, K0:V0],
+                                    scalar1=par[:, TAPS, HEADS + 1:HEADS + 2], scalar2=None, op0=ALU.mult)
+
+        x_codes = keep.tile([P, TILES, PASSES, P], U32, align_bytes=64)
+        x_scales = keep.tile([P, TILES, PASSES, P], U8, align_bytes=64)
+        w_codes = keep.tile([P, 3, PASSES, 512], U32, align_bytes=64)
+        w_scales = keep.tile([P, 3, PASSES, 512], U8, align_bytes=64)
+        turned = {}
+        grouped = {}
+
+        def turn(kind, i, tag):
+            raw = x_raw if kind == "x" else w_raw
+            words = raw[:, i, :].bitcast(F32)
+            t = bank(tag)
+            for g in range(PASSES):
+                for u in range(2):
+                    c = (2 * g + u) * P
+                    nc.tensor.transpose(t[:, c:c + P], words[:, 256 * g + u:256 * (g + 1):2], ident[:])
+            turned[kind, i] = t
+
+        def interleave(kind, i, on_vector):
+            src = turned[kind, i][:].rearrange("p (g u r) -> p g r u", g=PASSES, u=2)
+            if kind == "x":
+                xg = work.tile([P, PASSES * 4 * P], BF16, name="xg", tag="xg", bufs=4, align_bytes=64)
+                grouped[kind, i] = xg
+                dst = xg[:].bitcast(F32).rearrange("p (g r u) -> p g r u", g=PASSES, u=2)
+            else:
+                if i % 4 == 0:
+                    grouped[kind, i // 4] = work.tile([P, PASSES, 2048], BF16, name="wg", tag="wg", bufs=2, align_bytes=64)
+                r0 = 256 * (i % 4)
+                dst = grouped[kind, i // 4][:].bitcast(F32)[:, :, r0:r0 + 256].rearrange("p g (r u) -> p g r u", u=2)
+            if on_vector:
+                nc.vector.tensor_copy(out=dst, in_=src)
+            else:
+                nc.scalar.copy(out=dst, in_=src)
+
+        def quantize_x(i):
+            nc.vector.quantize_mx(
+                out=x_codes[:, i, :, :].rearrange("p g r -> p (g r)").bitcast(E5M2),
+                scales=x_scales[:, i, :, :].rearrange("p g r -> p (g r)"),
+                in_=grouped["x", i][:])
+
+        def quantize_w(grp, g):
+            nc.vector.quantize_mx(out=w_codes[:, grp, g, :].bitcast(E4M3), scales=w_scales[:, grp, g, :],
+                                  in_=grouped["w", grp][:, g, :])
+
+        items = {}
+        for b in range(BLOCKS):
+            for n in range(10):
+                items[HEADS * b - LEAD + n] = (b, n)
+        proj = {}
+        sums = {}
+        rstd = {}
+        normed = {}
+
+        def project(t):
+            b, n = items[t]
+            acc = bank("m%d" % (t % 3))
+            if n < 8:
+                parts = [(BLOCK_TILES * b + n % 4, n // 4, 0, 512)]
+            else:
+                parts = [(BLOCK_TILES * b + 2 * (n - 8) + e, 2, 256 * e, 256) for e in range(2)]
+            for i, grp, c0, width in parts:
+                for g in range(PASSES):
+                    nc.tensor.matmul_mx(
+                        out=acc[:, c0:c0 + width],
+                        lhsT=x_codes[:, i, g, :].bitcast(E5M2), lhsT_scale=x_scales[:, i, g, :],
+                        rhs=w_codes[:, grp, g, 0:width].bitcast(E4M3), rhs_scale=w_scales[:, grp, g, 0:width],
+                        start=(g == 0), stop=(g == PASSES - 1))
+            proj[t] = acc
+
+        def sum_squares(t):
+            ss = work.tile([P, 4], F32, name="ss", tag="ss", bufs=3)
+            squares = work.tile([P, 4, D], BF16, name="squares", tag="squares", bufs=2)
+            for e in range(4):
+                nc.scalar.activation(out=squares[:, e, :], in_=proj[t][:, e * D:(e + 1) * D], func=ACT.Square,
+                                     accum_out=ss[:, e:e + 1])
+            sums[t] = ss
+
+        def inverse_rms(t):
+            ms = work.tile([P, 4], F32, name="ms", tag="ms", bufs=2)
+            r = work.tile([P, 4], F32, name="r", tag="r", bufs=3)
+            nc.gpsimd.tensor_scalar(out=ms[:], in0=sums[t][:], scalar1=1.0 / D, scalar2=EPS, op0=ALU.mult, op1=ALU.add)
+            nc.gpsimd.tensor_tensor(out=r[:], in0=ms[:], in1=minus_half[:], op=ALU.pow)
+            rstd[t] = r
+
+        def normalise(t):
+            b, n = items[t]
+            grp = n // 4
+            if n % 4 == 0:
+                normed[b, grp] = work.tile([P, BLOCK_TILES, 512], F32, name="nb", tag="nb", bufs=3)
+            for e in range(4):
+                if n < 8:
+                    dst = normed[b, grp][:, n % 4, e * D:(e + 1) * D]
+                else:
+                    dst = normed[b, grp][:, 2 * (n - 8) + e // 2, (e % 2) * D:(e % 2 + 1) * D]
+                nc.scalar.activation(out=dst, in_=proj[t][:, e * D:(e + 1) * D], func=ACT.Copy,
+                                     scale=rstd[t][:, e:e + 1])
+
+        accs = [keep.tile([P, ACC_W], F32, name="acc%d" % h) for h in range(HEADS)]
+        chan = {}
+        us = {}
+        acts = {}
+        zs = {}
+        rot = {}
+        stage = {}
+
+        def to_channels(s):
+            b, h = divmod(s, HEADS)
+            t = bank("n%d" % (s % 3))
+            for i in range(BLOCK_TILES):
+                if h < V0:
+                    nc.tensor.transpose(t[:, i * P:(i + 1) * P], normed[b, h // 4][:, i, (h % 4) * D:(h % 4 + 1) * D], ident[:])
+                else:
+                    c0 = (h - K0) * D
+                    for g in range(PASSES):
+                        nc.tensor.matmul_mx(
+                            out=t[:, i * P:(i + 1) * P],
+                            lhsT=w_codes[:, 2, g, c0:c0 + D].bitcast(E4M3), lhsT_scale=w_scales[:, 2, g, c0:c0 + D],
+                            rhs=x_codes[:, BLOCK_TILES * b + i, g, :].bitcast(E5M2),
+                            rhs_scale=x_scales[:, BLOCK_TILES * b + i, g, :],
+                            start=(g == 0), stop=(g == PASSES - 1))
+            chan[s] = t
+
+        def copy_u(s):
+            h = s % HEADS
+            u = work.tile([P, BLOCK], F32, name="u", tag="u", bufs=4)
+            if h < V0:
+                col = HEADS if h < K0 else HEADS + 1
+                nc.scalar.activation(out=u[:], in_=chan[s][:], func=ACT.Copy, scale=par[:, TAPS, col:col + 1])
+            else:
+                nc.scalar.copy(out=u[:], in_=chan[s][:])
+            us[s] = u
+
+        def tap_width(b, shift):
+            return BLOCK - shift if b == BLOCKS - 1 else BLOCK
+
+        def first_tap(s):
+            b, h = divmod(s, HEADS)
+            if b == 0:
+                nc.gpsimd.memset(accs[h][:, 0:HALO], 0.0)
+            else:
+                nc.gpsimd.tensor_copy(out=accs[h][:, 0:HALO], in_=accs[h][:, BLOCK:BLOCK + HALO])
+            w = tap_width(b, HALO)
+            nc.gpsimd.tensor_scalar(out=accs[h][:, HALO:HALO + w], in0=us[s][:, 0:w], scalar1=par[:, 0, h:h + 1],
+                                    scalar2=0.0, op0=ALU.mult, op1=ALU.add)
+
+        def tap(s, j):
+            b, h = divmod(s, HEADS)
+            shift = HALO - j
+            w = tap_width(b, shift)
+            weight = tap_n[:, j - 1, h:h + 1] if h < V0 else par[:, j, h:h + 1]
+            nc.vector.scalar_tensor_tensor(out=accs[h][:, shift:shift + w], in0=chan[s][:, 0:w], scalar=weight,
+                                           in1=accs[h][:, shift:shift + w], op0=ALU.mult, op1=ALU.add)
+
+        def silu(s):
+            h = s % HEADS
+            a = work.tile([P, BLOCK], F32, name="a", tag="a", bufs=3)
+            nc.scalar.activation(out=a[:], in_=accs[h][:, 0:BLOCK], func=ACT.Silu, bias=par[:, TAPS, h:h + 1])
+            acts[s] = a
+
+        def to_tokens(s):
+            z = bank("z%d" % (s % 2))
+            for i in range(BLOCK_TILES):
+                cols = slice(i * P, (i + 1) * P)
+                nc.tensor.matmul(z[:, cols], lhsT=us[s][:, cols], rhs=ident[:], is_transpose=True, start=True, stop=False)
+                nc.tensor.matmul(z[:, cols], lhsT=acts[s][:, cols], rhs=ident[:], is_transpose=True, start=False, stop=True)
+            zs[s] = z
+
+        def unit(s):
+            b, h = divmod(s, HEADS)
+            first = [0, 0, 0, 0, 4, 4, 4, 4, 8, 8, 10, 10][h]
+            count = 4 if h < K0 else 2
+            return b, h, first, count
+
+        def staged(s):
+            b, h, first, count = unit(s)
+            if (b, first) not in stage:
+                stage[b, first] = work.tile([P, BLOCK_TILES, count * D], F32, name="st", tag="st", bufs=3)
+            return stage[b, first][:, :, (h - first) * D:(h - first + 1) * D]
+
+        def rope_cos(s):
+            b = s // HEADS
+            nc.vector.tensor_tensor(out=staged(s), in0=zs[s][:].rearrange("p (i d) -> p i d", d=D),
+                                    in1=cos_sb[:, BLOCK_TILES * b:BLOCK_TILES * (b + 1), :], op=ALU.mult)
+
+        def rope_sin(s):
+            b = s // HEADS
+            t = work.tile([P, BLOCK_TILES, D], F32, name="rot", tag="rot", bufs=3)
+            swapped = zs[s][:].rearrange("p (i e d) -> p i e d", e=2, d=D // 2)[:, :, ::-1, :]
+            nc.vector.tensor_tensor(
+                out=t[:].rearrange("p i (e d) -> p i e d", e=2), in0=swapped,
+                in1=sin_sb[:, BLOCK_TILES * b:BLOCK_TILES * (b + 1), :].rearrange("p i (e d) -> p i e d", e=2),
+                op=ALU.mult)
+            rot[s] = t
+
+        out_rows = [o.rearrange("b (i p) h d -> p (b i) (h d)", p=P) for o in (out_0, out_1, out_2)]
+
+        def store(s):
+            b, h, first, count = unit(s)
+            which = 0 if h < K0 else (1 if h < V0 else 2)
+            c0 = (first - (0, K0, V0)[which]) * D
+            tiles = slice(BLOCK_TILES * b, BLOCK_TILES * (b + 1))
+            if s >= STEPS - KV_HEADS:
+                e = h - first
+                nc.sync.dma_start(out=out_rows[which][:, tiles, e * D:(e + 1) * D], in_=staged(s))
+            elif h == first + count - 1:
+                nc.sync.dma_start(out=out_rows[which][:, tiles, c0:c0 + count * D], in_=stage[b, first][:])
+
+        def rope_add(s):
+            nc.gpsimd.tensor_tensor(out=staged(s), in0=staged(s), in1=rot[s][:], op=ALU.add)
+            store(s)
+
+        def copy_v(s):
+            nc.scalar.copy(out=staged(s), in_=zs[s][:].rearrange("p (i d) -> p i d", d=D))
+            store(s)
+
+        def live(s):
+            return 0 <= s < STEPS
+
+        def rotated(s):
+            return live(s) and s % HEADS < V0
+
+        spare = ["n0", "n1", "n2", "z0", "z1"]
+        for i in range(4):
+            turn("w", i, spare[i])
+            interleave("w", i, i % 2 == 0)
+        turn("x", 0, spare[4])
+        turn("x", 1, spare[0])
+        interleave("x", 0, False)
+        interleave("x", 1, False)
+        quantize_w(0, 0)
+        quantize_w(0, 1)
+        quantize_x(0)
+        quantize_x(1)
+        early = [("x", 2), ("x", 3)] + [("w", i) for i in range(4, HEADS)] + [("x", i) for i in range(4, 8)]
+        early_banks = ["n1", "n2", "z0", "z1", "n0", "n1", "n2", "z0", "z1", "n0", "z0", "z1", "z0", "z1"]
+        late_turn = {}
+        late_copy = {}
+        fill = {}
+        for b in range(BLOCKS - 2):
+            t = HEADS * b - LEAD + 10
+            i0 = BLOCK_TILES * (b + 2)
+            late_turn[t, "first"] = (i0, "m%d" % (t % 3))
+            late_turn[t + 1, "first"] = (i0 + 1, "m%d" % ((t + 1) % 3))
+            late_turn[t + 1, "last"] = (i0 + 2, "m%d" % (t % 3))
+            late_turn[t + 2, "last"] = (i0 + 3, "m%d" % ((t + 1) % 3))
+            late_copy[t + 1, "first"] = i0
+            late_copy[t + 2, "first"] = i0 + 1
+            late_copy[t + 2, "last"] = i0 + 2
+            late_copy[t + 3, "last"] = i0 + 3
+        for b in range(BLOCKS - 1):
+            i0 = BLOCK_TILES * (b + 1)
+            fill[HEADS * b] = [i0, i0 + 1]
+            fill[HEADS * b + 1] = [i0 + 2, i0 + 3]
+
+        for s in range(-LEAD, STEPS + 3):
+            if live(s + 1):
+                to_channels(s + 1)
+            if live(s - 1):
+                silu(s - 1)
+            if s in items:
+                project(s)
+            if (s, "first") in late_turn:
+                turn("x", *late_turn[s, "first"])
+            if live(s + 1):
+                copy_u(s + 1)
+            if live(s - 1):
+                to_tokens(s - 1)
+            if live(s - 2) and not rotated(s - 2):
+                copy_v(s - 2)
+            if s - 1 in items:
+                sum_squares(s - 1)
+            if (s, "first") in late_copy:
+                interleave("x", late_copy[s, "first"], False)
+            if (s, "last") in late_turn:
+                turn("x", *late_turn[s, "last"])
+            if s - 2 in items:
+                normalise(s - 2)
+            if (s, "last") in late_copy:
+                interleave("x", late_copy[s, "last"], False)
+            if rotated(s - 3):
+                rope_add(s - 3)
+            if live(s + 1):
+                first_tap(s + 1)
+            if s - 1 in items:
+                inverse_rms(s - 1)
+            if s < 0:
+                n = 2 * (s + LEAD)
+                if s == -2:
+                    constants("n1", "n2")
+                for e in range(2):
+                    turn(*early[n + e], early_banks[n + e])
+                for e in range(2):
+                    interleave(*early[n + e], True)
+                if s == -2:
+                    fold_norm_weights()
+                if s == -LEAD:
+                    quantize_x(2)
+                    quantize_x(3)
+                if s in (-5, -3):
+                    quantize_w((s + LEAD) // 2, 0)
+                    quantize_w((s + LEAD) // 2, 1)
+            if live(s):
+                tap(s, 1)
+            if rotated(s - 2):
+                rope_cos(s - 2)
+            if s in fill:
+                quantize_x(fill[s][0])
+            if live(s):
+                tap(s, 2)
+            if rotated(s - 2):
+                rope_sin(s - 2)
+            if s in fill:
+                quantize_x(fill[s][1])
+            if s == 1:
+                nc.vector.tensor_scalar(out=sin_sb[:, :, 0:D // 2], in0=sin_sb[:, :, 0:D // 2], scalar1=-1.0,
+                                        scalar2=None, op0=ALU.mult)
+            if live(s):
+                tap(s, 3)

@@ -29,8 +29,11 @@ HALO = TAPS - 1
 ACC_W = 520
 STEPS = BLOCKS * HEADS
 LEAD = 7
+U_BUFS = 4
 K0 = Q_HEADS
 V0 = Q_HEADS + KV_HEADS
+TINY = 2.0 ** -40
+TURN_STEPS = (-8, -5, -2, 1)
 
 
 def tile_attention_pa_kernel(tc, x, cos, sin, q_w, k_w, v_w, q_norm_w, k_norm_w,
@@ -54,8 +57,8 @@ def tile_attention_pa_kernel(tc, x, cos, sin, q_w, k_w, v_w, q_norm_w, k_norm_w,
         x_raw = keep.tile([P, TILES, HID], BF16)
         cos_sb = keep.tile([P, TILES, D], BF16)
         sin_sb = keep.tile([P, TILES, D], BF16)
-        nc.sync.dma_start(out=w_raw[:, 0:2, :], in_=q_rows[:, 0:2, :])
-        nc.sync.dma_start(out=w_raw[:, 2:4, :], in_=q_rows[:, 2:4, :])
+        nc.sync.dma_start(out=w_raw[:, 0:1, :], in_=q_rows[:, 0:1, :])
+        nc.sync.dma_start(out=w_raw[:, 1:4, :], in_=q_rows[:, 1:4, :])
         nc.sync.dma_start(out=x_raw[:, 0:2, :], in_=x_rows[:, 0:2, :])
         nc.sync.dma_start(out=x_raw[:, 2:4, :], in_=x_rows[:, 2:4, :])
         nc.sync.dma_start(out=w_raw[:, 4:8, :], in_=q_rows[:, 4:8, :])
@@ -79,7 +82,10 @@ def tile_attention_pa_kernel(tc, x, cos, sin, q_w, k_w, v_w, q_norm_w, k_norm_w,
         minus_half = keep.tile([P, 4], F32)
         nc.gpsimd.memset(minus_half[:], -0.5)
         par = keep.tile([P, TAPS + 1, 16], F32)
-        tap_n = keep.tile([P, TAPS - 1, V0], F32)
+        tap_n = keep.tile([P, HALO, HEADS], F32)
+        pivot = keep.tile([P, HEADS], F32)
+        small = keep.tile([P, HEADS], F32)
+        inverse = keep.tile([P, HEADS], F32)
 
         def constants(tag_a, tag_b):
             a = bank(tag_a)
@@ -91,9 +97,17 @@ def tile_attention_pa_kernel(tc, x, cos, sin, q_w, k_w, v_w, q_norm_w, k_norm_w,
             nc.vector.tensor_copy(out=par[:, TAPS, :], in_=b[:, 0:16])
 
         def fold_norm_weights():
-            nc.vector.tensor_scalar(out=tap_n[:, :, 0:K0], in0=par[:, 1:TAPS, 0:K0],
+            last = par[:, HALO, 0:HEADS]
+            nc.vector.tensor_tensor(out=small[:], in0=last, in1=last, op=ALU.mult)
+            nc.vector.tensor_scalar(out=small[:], in0=small[:], scalar1=TINY * TINY, scalar2=2.0 * TINY,
+                                    op0=ALU.is_lt, op1=ALU.mult)
+            nc.vector.tensor_tensor(out=pivot[:], in0=last, in1=small[:], op=ALU.add)
+            nc.vector.reciprocal(out=inverse[:], in_=pivot[:])
+            nc.vector.tensor_tensor(out=tap_n[:], in0=par[:, 0:HALO, 0:HEADS],
+                                    in1=inverse[:].unsqueeze(1).to_broadcast([P, HALO, HEADS]), op=ALU.mult)
+            nc.vector.tensor_scalar(out=tap_n[:, :, 0:K0], in0=tap_n[:, :, 0:K0],
                                     scalar1=par[:, TAPS, HEADS:HEADS + 1], scalar2=None, op0=ALU.mult)
-            nc.vector.tensor_scalar(out=tap_n[:, :, K0:V0], in0=par[:, 1:TAPS, K0:V0],
+            nc.vector.tensor_scalar(out=tap_n[:, :, K0:V0], in0=tap_n[:, :, K0:V0],
                                     scalar1=par[:, TAPS, HEADS + 1:HEADS + 2], scalar2=None, op0=ALU.mult)
 
         x_codes = keep.tile([P, TILES, PASSES, P], U32, align_bytes=64)
@@ -116,12 +130,12 @@ def tile_attention_pa_kernel(tc, x, cos, sin, q_w, k_w, v_w, q_norm_w, k_norm_w,
         def interleave(kind, i, on_vector):
             src = turned[kind, i][:].rearrange("p (g u r) -> p g r u", g=PASSES, u=2)
             if kind == "x":
-                xg = work.tile([P, PASSES * 4 * P], BF16, name="xg", tag="xg", bufs=4, align_bytes=64)
-                grouped[kind, i] = xg
-                dst = xg[:].bitcast(F32).rearrange("p (g r u) -> p g r u", g=PASSES, u=2)
+                if i % 4 == 0:
+                    grouped[kind, i // 4] = work.tile([P, BLOCK_TILES, HID], BF16, name="xg", tag="xg", bufs=1, align_bytes=64)
+                dst = grouped[kind, i // 4][:, i % 4, :].bitcast(F32).rearrange("p (g r u) -> p g r u", g=PASSES, u=2)
             else:
                 if i % 4 == 0:
-                    grouped[kind, i // 4] = work.tile([P, PASSES, 2048], BF16, name="wg", tag="wg", bufs=2, align_bytes=64)
+                    grouped[kind, i // 4] = work.tile([P, PASSES, 2048], BF16, name="wg", tag="wg", bufs=1, align_bytes=64)
                 r0 = 256 * (i % 4)
                 dst = grouped[kind, i // 4][:].bitcast(F32)[:, :, r0:r0 + 256].rearrange("p g (r u) -> p g r u", u=2)
             if on_vector:
@@ -129,11 +143,11 @@ def tile_attention_pa_kernel(tc, x, cos, sin, q_w, k_w, v_w, q_norm_w, k_norm_w,
             else:
                 nc.scalar.copy(out=dst, in_=src)
 
-        def quantize_x(i):
+        def quantize_x(i, count):
             nc.vector.quantize_mx(
-                out=x_codes[:, i, :, :].rearrange("p g r -> p (g r)").bitcast(E5M2),
-                scales=x_scales[:, i, :, :].rearrange("p g r -> p (g r)"),
-                in_=grouped["x", i][:])
+                out=x_codes[:, i:i + count, :, :].rearrange("p i g r -> p (i g r)").bitcast(E5M2),
+                scales=x_scales[:, i:i + count, :, :].rearrange("p i g r -> p (i g r)"),
+                in_=grouped["x", i // 4][:, i % 4:i % 4 + count, :].rearrange("p i k -> p (i k)"))
 
         def quantize_w(grp, g):
             nc.vector.quantize_mx(out=w_codes[:, grp, g, :].bitcast(E4M3), scales=w_scales[:, grp, g, :],
@@ -142,15 +156,15 @@ def tile_attention_pa_kernel(tc, x, cos, sin, q_w, k_w, v_w, q_norm_w, k_norm_w,
         items = {}
         for b in range(BLOCKS):
             for n in range(10):
-                items[HEADS * b - LEAD + n] = (b, n)
+                items[HEADS * b - LEAD + n + (2 if n >= 8 else 0)] = (b, n)
         proj = {}
         sums = {}
         rstd = {}
         normed = {}
 
-        def project(t):
+        def project(t, tag=None):
             b, n = items[t]
-            acc = bank("m%d" % (t % 3))
+            acc = bank(tag or "m%d" % (t % 3))
             if n < 8:
                 parts = [(BLOCK_TILES * b + n % 4, n // 4, 0, 512)]
             else:
@@ -170,13 +184,13 @@ def tile_attention_pa_kernel(tc, x, cos, sin, q_w, k_w, v_w, q_norm_w, k_norm_w,
             for e in range(4):
                 nc.scalar.activation(out=squares[:, e, :], in_=proj[t][:, e * D:(e + 1) * D], func=ACT.Square,
                                      accum_out=ss[:, e:e + 1])
-            sums[t] = ss
+            ms = work.tile([P, 4], F32, name="ms", tag="ms", bufs=3)
+            nc.scalar.activation(out=ms[:], in_=ss[:], func=ACT.Copy, scale=1.0 / D, bias=EPS)
+            sums[t] = ms
 
         def inverse_rms(t):
-            ms = work.tile([P, 4], F32, name="ms", tag="ms", bufs=2)
-            r = work.tile([P, 4], F32, name="r", tag="r", bufs=3)
-            nc.gpsimd.tensor_scalar(out=ms[:], in0=sums[t][:], scalar1=1.0 / D, scalar2=EPS, op0=ALU.mult, op1=ALU.add)
-            nc.gpsimd.tensor_tensor(out=r[:], in0=ms[:], in1=minus_half[:], op=ALU.pow)
+            r = work.tile([P, 4], F32, name="r", tag="r", bufs=4)
+            nc.gpsimd.tensor_tensor(out=r[:], in0=sums[t][:], in1=minus_half[:], op=ALU.pow)
             rstd[t] = r
 
         def normalise(t):
@@ -192,7 +206,11 @@ def tile_attention_pa_kernel(tc, x, cos, sin, q_w, k_w, v_w, q_norm_w, k_norm_w,
                 nc.scalar.activation(out=dst, in_=proj[t][:, e * D:(e + 1) * D], func=ACT.Copy,
                                      scale=rstd[t][:, e:e + 1])
 
-        accs = [keep.tile([P, ACC_W], F32, name="acc%d" % h) for h in range(HEADS)]
+        acc_all = keep.tile([P, HEADS, ACC_W], F32)
+        nc.gpsimd.memset(acc_all[:, :, BLOCK:BLOCK + HALO], 0.0)
+        u_all = keep.tile([P, U_BUFS, ACC_W], F32)
+        nc.gpsimd.memset(u_all[:, :, BLOCK:BLOCK + HALO], 0.0)
+        accs = [acc_all[:, h, :] for h in range(HEADS)]
         chan = {}
         us = {}
         acts = {}
@@ -202,7 +220,7 @@ def tile_attention_pa_kernel(tc, x, cos, sin, q_w, k_w, v_w, q_norm_w, k_norm_w,
 
         def to_channels(s):
             b, h = divmod(s, HEADS)
-            t = bank("n%d" % (s % 3))
+            t = bank("n%d" % (s % 2))
             for i in range(BLOCK_TILES):
                 if h < V0:
                     nc.tensor.transpose(t[:, i * P:(i + 1) * P], normed[b, h // 4][:, i, (h % 4) * D:(h % 4 + 1) * D], ident[:])
@@ -219,39 +237,32 @@ def tile_attention_pa_kernel(tc, x, cos, sin, q_w, k_w, v_w, q_norm_w, k_norm_w,
 
         def copy_u(s):
             h = s % HEADS
-            u = work.tile([P, BLOCK], F32, name="u", tag="u", bufs=4)
+            u = u_all[:, s % U_BUFS, :]
             if h < V0:
                 col = HEADS if h < K0 else HEADS + 1
-                nc.scalar.activation(out=u[:], in_=chan[s][:], func=ACT.Copy, scale=par[:, TAPS, col:col + 1])
+                nc.scalar.activation(out=u[:, 0:BLOCK], in_=chan[s][:], func=ACT.Copy, scale=par[:, TAPS, col:col + 1])
             else:
-                nc.scalar.copy(out=u[:], in_=chan[s][:])
+                nc.scalar.copy(out=u[:, 0:BLOCK], in_=chan[s][:])
             us[s] = u
 
-        def tap_width(b, shift):
-            return BLOCK - shift if b == BLOCKS - 1 else BLOCK
-
-        def first_tap(s):
-            b, h = divmod(s, HEADS)
-            if b == 0:
-                nc.gpsimd.memset(accs[h][:, 0:HALO], 0.0)
-            else:
-                nc.gpsimd.tensor_copy(out=accs[h][:, 0:HALO], in_=accs[h][:, BLOCK:BLOCK + HALO])
-            w = tap_width(b, HALO)
-            nc.gpsimd.tensor_scalar(out=accs[h][:, HALO:HALO + w], in0=us[s][:, 0:w], scalar1=par[:, 0, h:h + 1],
-                                    scalar2=0.0, op0=ALU.mult, op1=ALU.add)
+        def carry(s):
+            h = s % HEADS
+            nc.gpsimd.tensor_tensor(out=accs[h][:, 0:HALO], in0=accs[h][:, BLOCK:BLOCK + HALO], in1=us[s][:, 0:HALO],
+                                    op=ALU.add)
 
         def tap(s, j):
-            b, h = divmod(s, HEADS)
+            h = s % HEADS
             shift = HALO - j
-            w = tap_width(b, shift)
-            weight = tap_n[:, j - 1, h:h + 1] if h < V0 else par[:, j, h:h + 1]
-            nc.vector.scalar_tensor_tensor(out=accs[h][:, shift:shift + w], in0=chan[s][:, 0:w], scalar=weight,
-                                           in1=accs[h][:, shift:shift + w], op0=ALU.mult, op1=ALU.add)
+            w = BLOCK
+            onto = us[s] if j == 0 else accs[h]
+            nc.vector.scalar_tensor_tensor(out=accs[h][:, shift:shift + w], in0=chan[s][:, 0:w], scalar=tap_n[:, j, h:h + 1],
+                                           in1=onto[:, shift:shift + w], op0=ALU.mult, op1=ALU.add)
 
         def silu(s):
             h = s % HEADS
             a = work.tile([P, BLOCK], F32, name="a", tag="a", bufs=3)
-            nc.scalar.activation(out=a[:], in_=accs[h][:, 0:BLOCK], func=ACT.Silu, bias=par[:, TAPS, h:h + 1])
+            nc.scalar.activation(out=a[:], in_=accs[h][:, 0:BLOCK], func=ACT.Silu, scale=pivot[:, h:h + 1],
+                                 bias=par[:, TAPS, h:h + 1])
             acts[s] = a
 
         def to_tokens(s):
@@ -307,7 +318,7 @@ def tile_attention_pa_kernel(tc, x, cos, sin, q_w, k_w, v_w, q_norm_w, k_norm_w,
             store(s)
 
         def copy_v(s):
-            nc.scalar.copy(out=staged(s), in_=zs[s][:].rearrange("p (i d) -> p i d", d=D))
+            nc.vector.tensor_copy(out=staged(s), in_=zs[s][:].rearrange("p (i d) -> p i d", d=D))
             store(s)
 
         def live(s):
@@ -316,100 +327,93 @@ def tile_attention_pa_kernel(tc, x, cos, sin, q_w, k_w, v_w, q_norm_w, k_norm_w,
         def rotated(s):
             return live(s) and s % HEADS < V0
 
-        spare = ["n0", "n1", "n2", "z0", "z1"]
         for i in range(4):
-            turn("w", i, spare[i])
+            turn("w", i, ["n0", "n1", "t", "z0"][i])
             interleave("w", i, i % 2 == 0)
-        turn("x", 0, spare[4])
-        turn("x", 1, spare[0])
-        interleave("x", 0, False)
-        interleave("x", 1, False)
+        for i in range(4):
+            turn("x", i, ["z1", "n0", "n1", "t"][i])
         quantize_w(0, 0)
+        interleave("x", 0, False)
         quantize_w(0, 1)
-        quantize_x(0)
-        quantize_x(1)
-        early = [("x", 2), ("x", 3)] + [("w", i) for i in range(4, HEADS)] + [("x", i) for i in range(4, 8)]
-        early_banks = ["n1", "n2", "z0", "z1", "n0", "n1", "n2", "z0", "z1", "n0", "z0", "z1", "z0", "z1"]
-        late_turn = {}
-        late_copy = {}
+        interleave("x", 1, False)
+        quantize_x(0, 1)
+        interleave("x", 2, True)
+        quantize_x(1, 1)
+        interleave("x", 3, False)
+        quantize_x(2, 1)
+        quantize_x(3, 1)
+        constants("z0", "z1")
+        fold_norm_weights()
+        for n in range(4):
+            project(n - LEAD, ["m0", "m1", "m2", "n0"][n])
+            sum_squares(n - LEAD)
+            inverse_rms(n - LEAD)
+        for i in range(4, 8):
+            turn("w", i, ["n1", "t", "z0", "z1"][i - 4])
+            interleave("w", i, True)
+        quantize_w(1, 0)
+        quantize_w(1, 1)
+        for n in range(4):
+            normalise(n - LEAD)
+        for i in range(8, 10):
+            turn("w", i, ["z0", "z1"][i - 8])
+            interleave("w", i, True)
+        to_channels(0)
+        copy_u(0)
+        carry(0)
+        first_item = 4 - LEAD
+        late = {}
         fill = {}
-        for b in range(BLOCKS - 2):
-            t = HEADS * b - LEAD + 10
-            i0 = BLOCK_TILES * (b + 2)
-            late_turn[t, "first"] = (i0, "m%d" % (t % 3))
-            late_turn[t + 1, "first"] = (i0 + 1, "m%d" % ((t + 1) % 3))
-            late_turn[t + 1, "last"] = (i0 + 2, "m%d" % (t % 3))
-            late_turn[t + 2, "last"] = (i0 + 3, "m%d" % ((t + 1) % 3))
-            late_copy[t + 1, "first"] = i0
-            late_copy[t + 2, "first"] = i0 + 1
-            late_copy[t + 2, "last"] = i0 + 2
-            late_copy[t + 3, "last"] = i0 + 3
         for b in range(BLOCKS - 1):
-            i0 = BLOCK_TILES * (b + 1)
-            fill[HEADS * b] = [i0, i0 + 1]
-            fill[HEADS * b + 1] = [i0 + 2, i0 + 3]
+            for i in range(BLOCK_TILES):
+                late[max(HEADS * b + TURN_STEPS[i], i - 2)] = BLOCK_TILES * (b + 1) + i
+            fill[HEADS * b + 2] = BLOCK_TILES * (b + 1)
 
-        for s in range(-LEAD, STEPS + 3):
-            if live(s + 1):
+        for s in range(first_item, STEPS + 3):
+            if live(s + 1) and s >= 0:
                 to_channels(s + 1)
             if live(s - 1):
                 silu(s - 1)
             if s in items:
                 project(s)
-            if (s, "first") in late_turn:
-                turn("x", *late_turn[s, "first"])
-            if live(s + 1):
+            if s in late:
+                turn("x", late[s], "t")
+            if live(s + 1) and s >= 0:
                 copy_u(s + 1)
             if live(s - 1):
                 to_tokens(s - 1)
-            if live(s - 2) and not rotated(s - 2):
-                copy_v(s - 2)
-            if s - 1 in items:
+            if s - 1 in items and s - 1 >= first_item:
                 sum_squares(s - 1)
-            if (s, "first") in late_copy:
-                interleave("x", late_copy[s, "first"], False)
-            if (s, "last") in late_turn:
-                turn("x", *late_turn[s, "last"])
-            if s - 2 in items:
+            if s - 2 in items and s - 2 >= first_item:
                 normalise(s - 2)
-            if (s, "last") in late_copy:
-                interleave("x", late_copy[s, "last"], False)
+            if s in late:
+                interleave("x", late[s], False)
             if rotated(s - 3):
                 rope_add(s - 3)
-            if live(s + 1):
-                first_tap(s + 1)
-            if s - 1 in items:
+            if live(s + 1) and s >= 0:
+                carry(s + 1)
+            if s - 1 in items and s - 1 >= first_item:
                 inverse_rms(s - 1)
-            if s < 0:
-                n = 2 * (s + LEAD)
-                if s == -2:
-                    constants("n1", "n2")
-                for e in range(2):
-                    turn(*early[n + e], early_banks[n + e])
-                for e in range(2):
-                    interleave(*early[n + e], True)
-                if s == -2:
-                    fold_norm_weights()
-                if s == -LEAD:
-                    quantize_x(2)
-                    quantize_x(3)
-                if s in (-5, -3):
-                    quantize_w((s + LEAD) // 2, 0)
-                    quantize_w((s + LEAD) // 2, 1)
+            if s == -2:
+                for i in range(10, 12):
+                    turn("w", i, ["z0", "z1"][i - 10])
+                    interleave("w", i, True)
+            if live(s):
+                tap(s, 0)
+            if rotated(s - 2):
+                rope_cos(s - 2)
+            if live(s - 2) and not rotated(s - 2):
+                copy_v(s - 2)
+            if s in (0, 1):
+                quantize_w(2, s)
             if live(s):
                 tap(s, 1)
             if rotated(s - 2):
-                rope_cos(s - 2)
-            if s in fill:
-                quantize_x(fill[s][0])
-            if live(s):
-                tap(s, 2)
-            if rotated(s - 2):
                 rope_sin(s - 2)
-            if s in fill:
-                quantize_x(fill[s][1])
             if s == 1:
                 nc.vector.tensor_scalar(out=sin_sb[:, :, 0:D // 2], in0=sin_sb[:, :, 0:D // 2], scalar1=-1.0,
                                         scalar2=None, op0=ALU.mult)
             if live(s):
-                tap(s, 3)
+                tap(s, 2)
+            if s in fill:
+                quantize_x(fill[s], BLOCK_TILES)

@@ -27,13 +27,14 @@ BLOCK = BLOCK_TILES * P
 BLOCKS = S // BLOCK
 HALO = TAPS - 1
 ACC_W = 520
-STEPS = BLOCKS * HEADS
-LEAD = 7
-U_BUFS = 4
 K0 = Q_HEADS
 V0 = Q_HEADS + KV_HEADS
+STEPS = BLOCKS * V0
+LEAD = 6
+V_START = (1, 6)
+V_START_LAST = (1, 4)
+U_BUFS = 4
 TINY = 2.0 ** -40
-TURN_STEPS = (-8, -5, -2, 1)
 
 
 def tile_attention_pa_kernel(tc, x, cos, sin, q_w, k_w, v_w, q_norm_w, k_norm_w,
@@ -82,10 +83,10 @@ def tile_attention_pa_kernel(tc, x, cos, sin, q_w, k_w, v_w, q_norm_w, k_norm_w,
         minus_half = keep.tile([P, 4], F32)
         nc.gpsimd.memset(minus_half[:], -0.5)
         par = keep.tile([P, TAPS + 1, 16], F32)
-        tap_n = keep.tile([P, HALO, HEADS], F32)
-        pivot = keep.tile([P, HEADS], F32)
-        small = keep.tile([P, HEADS], F32)
-        inverse = keep.tile([P, HEADS], F32)
+        tap_n = keep.tile([P, HALO, V0], F32)
+        pivot = keep.tile([P, V0], F32)
+        small = keep.tile([P, V0], F32)
+        inverse = keep.tile([P, V0], F32)
 
         def constants(tag_a, tag_b):
             a = bank(tag_a)
@@ -96,15 +97,23 @@ def tile_attention_pa_kernel(tc, x, cos, sin, q_w, k_w, v_w, q_norm_w, k_norm_w,
             nc.vector.tensor_copy(out=par[:, 0:TAPS, :], in_=a[:].rearrange("p (j c) -> p j c", j=TAPS)[:, :, 0:16])
             nc.vector.tensor_copy(out=par[:, TAPS, :], in_=b[:, 0:16])
 
+        diag = keep.tile([P, KV_HEADS, TAPS, P], F32)
+
+        def tap_diagonals():
+            for e in range(KV_HEADS):
+                for j in range(TAPS):
+                    nc.vector.tensor_scalar(out=diag[:, e, j, :], in0=ident[:], scalar1=par[:, j, V0 + e:V0 + e + 1],
+                                            scalar2=None, op0=ALU.mult)
+
         def fold_norm_weights():
-            last = par[:, HALO, 0:HEADS]
+            last = par[:, HALO, 0:V0]
             nc.vector.tensor_tensor(out=small[:], in0=last, in1=last, op=ALU.mult)
             nc.vector.tensor_scalar(out=small[:], in0=small[:], scalar1=TINY * TINY, scalar2=2.0 * TINY,
                                     op0=ALU.is_lt, op1=ALU.mult)
             nc.vector.tensor_tensor(out=pivot[:], in0=last, in1=small[:], op=ALU.add)
             nc.vector.reciprocal(out=inverse[:], in_=pivot[:])
-            nc.vector.tensor_tensor(out=tap_n[:], in0=par[:, 0:HALO, 0:HEADS],
-                                    in1=inverse[:].unsqueeze(1).to_broadcast([P, HALO, HEADS]), op=ALU.mult)
+            nc.vector.tensor_tensor(out=tap_n[:], in0=par[:, 0:HALO, 0:V0],
+                                    in1=inverse[:].unsqueeze(1).to_broadcast([P, HALO, V0]), op=ALU.mult)
             nc.vector.tensor_scalar(out=tap_n[:, :, 0:K0], in0=tap_n[:, :, 0:K0],
                                     scalar1=par[:, TAPS, HEADS:HEADS + 1], scalar2=None, op0=ALU.mult)
             nc.vector.tensor_scalar(out=tap_n[:, :, K0:V0], in0=tap_n[:, :, K0:V0],
@@ -156,7 +165,7 @@ def tile_attention_pa_kernel(tc, x, cos, sin, q_w, k_w, v_w, q_norm_w, k_norm_w,
         items = {}
         for b in range(BLOCKS):
             for n in range(10):
-                items[HEADS * b - LEAD + n + (2 if n >= 8 else 0)] = (b, n)
+                items[V0 * b - LEAD + n] = (b, n)
         proj = {}
         sums = {}
         rstd = {}
@@ -164,7 +173,7 @@ def tile_attention_pa_kernel(tc, x, cos, sin, q_w, k_w, v_w, q_norm_w, k_norm_w,
 
         def project(t, tag=None):
             b, n = items[t]
-            acc = bank(tag or "m%d" % (t % 3))
+            acc = bank(tag or "m%d" % (t % 2))
             if n < 8:
                 parts = [(BLOCK_TILES * b + n % 4, n // 4, 0, 512)]
             else:
@@ -206,78 +215,62 @@ def tile_attention_pa_kernel(tc, x, cos, sin, q_w, k_w, v_w, q_norm_w, k_norm_w,
                 nc.scalar.activation(out=dst, in_=proj[t][:, e * D:(e + 1) * D], func=ACT.Copy,
                                      scale=rstd[t][:, e:e + 1])
 
-        acc_all = keep.tile([P, HEADS, ACC_W], F32)
+        acc_all = keep.tile([P, V0, ACC_W], F32)
         nc.gpsimd.memset(acc_all[:, :, BLOCK:BLOCK + HALO], 0.0)
         u_all = keep.tile([P, U_BUFS, ACC_W], F32)
         nc.gpsimd.memset(u_all[:, :, BLOCK:BLOCK + HALO], 0.0)
-        accs = [acc_all[:, h, :] for h in range(HEADS)]
+        accs = [acc_all[:, h, :] for h in range(V0)]
         chan = {}
         us = {}
         acts = {}
         zs = {}
         rot = {}
         stage = {}
+        out_rows = [o.rearrange("b (i p) h d -> p (b i) (h d)", p=P) for o in (out_0, out_1, out_2)]
 
         def to_channels(s):
-            b, h = divmod(s, HEADS)
+            b, h = divmod(s, V0)
             t = bank("n%d" % (s % 2))
             for i in range(BLOCK_TILES):
-                if h < V0:
-                    nc.tensor.transpose(t[:, i * P:(i + 1) * P], normed[b, h // 4][:, i, (h % 4) * D:(h % 4 + 1) * D], ident[:])
-                else:
-                    c0 = (h - K0) * D
-                    for g in range(PASSES):
-                        nc.tensor.matmul_mx(
-                            out=t[:, i * P:(i + 1) * P],
-                            lhsT=w_codes[:, 2, g, c0:c0 + D].bitcast(E4M3), lhsT_scale=w_scales[:, 2, g, c0:c0 + D],
-                            rhs=x_codes[:, BLOCK_TILES * b + i, g, :].bitcast(E5M2),
-                            rhs_scale=x_scales[:, BLOCK_TILES * b + i, g, :],
-                            start=(g == 0), stop=(g == PASSES - 1))
+                nc.tensor.transpose(t[:, i * P:(i + 1) * P], normed[b, h // 4][:, i, (h % 4) * D:(h % 4 + 1) * D], ident[:])
             chan[s] = t
 
         def copy_u(s):
-            h = s % HEADS
+            h = s % V0
             u = u_all[:, s % U_BUFS, :]
-            if h < V0:
-                col = HEADS if h < K0 else HEADS + 1
-                nc.scalar.activation(out=u[:, 0:BLOCK], in_=chan[s][:], func=ACT.Copy, scale=par[:, TAPS, col:col + 1])
-            else:
-                nc.scalar.copy(out=u[:, 0:BLOCK], in_=chan[s][:])
+            col = HEADS if h < K0 else HEADS + 1
+            nc.scalar.activation(out=u[:, 0:BLOCK], in_=chan[s][:], func=ACT.Copy, scale=par[:, TAPS, col:col + 1])
             us[s] = u
 
         def carry(s):
-            h = s % HEADS
+            h = s % V0
             nc.gpsimd.tensor_tensor(out=accs[h][:, 0:HALO], in0=accs[h][:, BLOCK:BLOCK + HALO], in1=us[s][:, 0:HALO],
                                     op=ALU.add)
 
         def tap(s, j):
-            h = s % HEADS
+            h = s % V0
             shift = HALO - j
             w = BLOCK
             onto = us[s] if j == 0 else accs[h]
             nc.vector.scalar_tensor_tensor(out=accs[h][:, shift:shift + w], in0=chan[s][:, 0:w], scalar=tap_n[:, j, h:h + 1],
                                            in1=onto[:, shift:shift + w], op0=ALU.mult, op1=ALU.add)
 
-        def silu(s):
-            h = s % HEADS
-            a = work.tile([P, BLOCK], F32, name="a", tag="a", bufs=3)
-            nc.scalar.activation(out=a[:], in_=accs[h][:, 0:BLOCK], func=ACT.Silu, scale=pivot[:, h:h + 1],
-                                 bias=par[:, TAPS, h:h + 1])
-            acts[s] = a
+        def silu(pre, h, scale):
+            a = work.tile([P, BLOCK], F32, name="a", tag="a", bufs=4)
+            nc.scalar.activation(out=a[:], in_=pre, func=ACT.Silu, scale=scale, bias=par[:, TAPS, h:h + 1])
+            return a
 
-        def to_tokens(s):
-            z = bank("z%d" % (s % 2))
+        def to_tokens(u, a, tag):
+            z = bank(tag)
             for i in range(BLOCK_TILES):
                 cols = slice(i * P, (i + 1) * P)
-                nc.tensor.matmul(z[:, cols], lhsT=us[s][:, cols], rhs=ident[:], is_transpose=True, start=True, stop=False)
-                nc.tensor.matmul(z[:, cols], lhsT=acts[s][:, cols], rhs=ident[:], is_transpose=True, start=False, stop=True)
-            zs[s] = z
+                nc.tensor.matmul(z[:, cols], lhsT=u[:, cols], rhs=ident[:], is_transpose=True, start=True, stop=False)
+                nc.tensor.matmul(z[:, cols], lhsT=a[:, cols], rhs=ident[:], is_transpose=True, start=False, stop=True)
+            return z
 
         def unit(s):
-            b, h = divmod(s, HEADS)
-            first = [0, 0, 0, 0, 4, 4, 4, 4, 8, 8, 10, 10][h]
-            count = 4 if h < K0 else 2
-            return b, h, first, count
+            b, h = divmod(s, V0)
+            return b, h, h - h % 4, 4 if h < K0 else KV_HEADS
 
         def staged(s):
             b, h, first, count = unit(s)
@@ -286,12 +279,12 @@ def tile_attention_pa_kernel(tc, x, cos, sin, q_w, k_w, v_w, q_norm_w, k_norm_w,
             return stage[b, first][:, :, (h - first) * D:(h - first + 1) * D]
 
         def rope_cos(s):
-            b = s // HEADS
+            b = s // V0
             nc.vector.tensor_tensor(out=staged(s), in0=zs[s][:].rearrange("p (i d) -> p i d", d=D),
                                     in1=cos_sb[:, BLOCK_TILES * b:BLOCK_TILES * (b + 1), :], op=ALU.mult)
 
         def rope_sin(s):
-            b = s // HEADS
+            b = s // V0
             t = work.tile([P, BLOCK_TILES, D], F32, name="rot", tag="rot", bufs=3)
             swapped = zs[s][:].rearrange("p (i e d) -> p i e d", e=2, d=D // 2)[:, :, ::-1, :]
             nc.vector.tensor_tensor(
@@ -300,38 +293,78 @@ def tile_attention_pa_kernel(tc, x, cos, sin, q_w, k_w, v_w, q_norm_w, k_norm_w,
                 op=ALU.mult)
             rot[s] = t
 
-        out_rows = [o.rearrange("b (i p) h d -> p (b i) (h d)", p=P) for o in (out_0, out_1, out_2)]
-
-        def store(s):
+        def rope_add(s):
+            engine = nc.vector if s == STEPS - 1 else nc.gpsimd
+            engine.tensor_tensor(out=staged(s), in0=staged(s), in1=rot[s][:], op=ALU.add)
             b, h, first, count = unit(s)
-            which = 0 if h < K0 else (1 if h < V0 else 2)
-            c0 = (first - (0, K0, V0)[which]) * D
             tiles = slice(BLOCK_TILES * b, BLOCK_TILES * (b + 1))
             if s >= STEPS - KV_HEADS:
                 e = h - first
-                nc.sync.dma_start(out=out_rows[which][:, tiles, e * D:(e + 1) * D], in_=staged(s))
+                nc.sync.dma_start(out=out_rows[1][:, tiles, e * D:(e + 1) * D], in_=staged(s))
             elif h == first + count - 1:
+                which, c0 = (0, first * D) if h < K0 else (1, 0)
                 nc.sync.dma_start(out=out_rows[which][:, tiles, c0:c0 + count * D], in_=stage[b, first][:])
 
-        def rope_add(s):
-            nc.gpsimd.tensor_tensor(out=staged(s), in0=staged(s), in1=rot[s][:], op=ALU.add)
-            store(s)
+        v_bank = {}
+        v_u = {}
+        v_act = {}
 
-        def copy_v(s):
-            nc.vector.tensor_copy(out=staged(s), in_=zs[s][:].rearrange("p (i d) -> p i d", d=D))
-            store(s)
+        def v_project(b, e):
+            t = bank("v%d" % e)
+            c0 = (KV_HEADS + e) * D
+            for i in range(BLOCK_TILES):
+                for g in range(PASSES):
+                    nc.tensor.matmul_mx(
+                        out=t[:, i * P:(i + 1) * P],
+                        lhsT=w_codes[:, 2, g, c0:c0 + D].bitcast(E4M3), lhsT_scale=w_scales[:, 2, g, c0:c0 + D],
+                        rhs=x_codes[:, BLOCK_TILES * b + i, g, :].bitcast(E5M2),
+                        rhs_scale=x_scales[:, BLOCK_TILES * b + i, g, :],
+                        start=(g == 0), stop=(g == PASSES - 1))
+            v_bank[b, e] = t
+
+        def v_halo(b, e):
+            u = work.tile([P, ACC_W], F32, name="uv", tag="uv", bufs=3)
+            if b == 0:
+                nc.gpsimd.memset(u[:, 0:HALO], 0.0)
+            else:
+                nc.gpsimd.tensor_copy(out=u[:, 0:HALO], in_=v_u[b - 1, e][:, BLOCK:BLOCK + HALO])
+            v_u[b, e] = u
+
+        def v_copy_u(b, e):
+            nc.scalar.copy(out=v_u[b, e][:, HALO:HALO + BLOCK], in_=v_bank[b, e][:])
+
+        def v_tap(b, e, j):
+            if j == 0:
+                v_bank[b, e] = bank("v%d" % e)
+            nc.tensor.matmul(v_bank[b, e][:], lhsT=diag[:, e, j, :], rhs=v_u[b, e][:, j:j + BLOCK],
+                             start=(j == 0), stop=(j == TAPS - 1))
+
+        def v_store(b, e):
+            st = work.tile([P, BLOCK_TILES, D], F32, name="stv", tag="stv", bufs=2)
+            nc.vector.tensor_copy(out=st[:], in_=v_bank[b, e][:].rearrange("p (i d) -> p i d", d=D))
+            nc.sync.dma_start(out=out_rows[2][:, BLOCK_TILES * b:BLOCK_TILES * (b + 1), e * D:(e + 1) * D], in_=st[:])
+
+        v_phase = {}
+        late = {}
+        for b in range(BLOCKS):
+            for e in range(KV_HEADS):
+                for phase in range(7):
+                    v_phase.setdefault(V0 * b + (V_START if b < BLOCKS - 1 else V_START_LAST)[e] + phase, []).append((b, e, phase))
+        for b in range(1, BLOCKS):
+            for i in range(BLOCK_TILES):
+                late[V0 * (b - 1) + (-2, -1, 3, 4)[i]] = (BLOCK_TILES * b + i, "v%d" % (i // 2))
+
+        def v_in(s, phase):
+            return [(b, e) for b, e, p in v_phase.get(s, []) if p == phase]
 
         def live(s):
             return 0 <= s < STEPS
 
-        def rotated(s):
-            return live(s) and s % HEADS < V0
-
         for i in range(4):
-            turn("w", i, ["n0", "n1", "t", "z0"][i])
+            turn("w", i, ["n0", "n1", "z0", "z1"][i])
             interleave("w", i, i % 2 == 0)
         for i in range(4):
-            turn("x", i, ["z1", "n0", "n1", "t"][i])
+            turn("x", i, ["v0", "v1", "n0", "n1"][i])
         quantize_w(0, 0)
         interleave("x", 0, False)
         quantize_w(0, 1)
@@ -344,76 +377,84 @@ def tile_attention_pa_kernel(tc, x, cos, sin, q_w, k_w, v_w, q_norm_w, k_norm_w,
         quantize_x(3, 1)
         constants("z0", "z1")
         fold_norm_weights()
+        tap_diagonals()
         for n in range(4):
-            project(n - LEAD, ["m0", "m1", "m2", "n0"][n])
+            project(n - LEAD, ["m0", "m1", "v0", "v1"][n])
             sum_squares(n - LEAD)
             inverse_rms(n - LEAD)
         for i in range(4, 8):
-            turn("w", i, ["n1", "t", "z0", "z1"][i - 4])
+            turn("w", i, ["n0", "n1", "z0", "z1"][i - 4])
             interleave("w", i, True)
         quantize_w(1, 0)
         quantize_w(1, 1)
         for n in range(4):
             normalise(n - LEAD)
-        for i in range(8, 10):
-            turn("w", i, ["z0", "z1"][i - 8])
+        for i in range(8, 11):
+            turn("w", i, ["n1", "z0", "z1"][i - 8])
             interleave("w", i, True)
         to_channels(0)
         copy_u(0)
         carry(0)
+        turn("w", 11, "v1")
+        interleave("w", 11, False)
         first_item = 4 - LEAD
-        late = {}
-        fill = {}
-        for b in range(BLOCKS - 1):
-            for i in range(BLOCK_TILES):
-                late[max(HEADS * b + TURN_STEPS[i], i - 2)] = BLOCK_TILES * (b + 1) + i
-            fill[HEADS * b + 2] = BLOCK_TILES * (b + 1)
+
+        def streamed(t):
+            return t in items and t >= first_item
 
         for s in range(first_item, STEPS + 3):
             if live(s + 1) and s >= 0:
                 to_channels(s + 1)
             if live(s - 1):
-                silu(s - 1)
-            if s in items:
+                h = (s - 1) % V0
+                acts[s - 1] = silu(accs[h][:, 0:BLOCK], h, pivot[:, h:h + 1])
+            if streamed(s):
                 project(s)
-            if s in late:
-                turn("x", late[s], "t")
+            if live(s - 1):
+                zs[s - 1] = to_tokens(us[s - 1], acts[s - 1], "z%d" % ((s - 1) % 2))
             if live(s + 1) and s >= 0:
                 copy_u(s + 1)
-            if live(s - 1):
-                to_tokens(s - 1)
-            if s - 1 in items and s - 1 >= first_item:
-                sum_squares(s - 1)
-            if s - 2 in items and s - 2 >= first_item:
-                normalise(s - 2)
-            if s in late:
-                interleave("x", late[s], False)
-            if rotated(s - 3):
+            for b, e in v_in(s, 0):
+                v_project(b, e)
+                v_halo(b, e)
+            for b, e in v_in(s, 1):
+                v_copy_u(b, e)
+            for j in range(TAPS):
+                for b, e in v_in(s, 1 + j):
+                    v_tap(b, e, j)
+            for b, e in v_in(s, 5):
+                v_act[b, e] = silu(v_bank[b, e][:], V0 + e, 1.0)
+                v_bank[b, e] = to_tokens(v_u[b, e][:, HALO:HALO + BLOCK], v_act[b, e], "v%d" % e)
+            if streamed(s):
+                sum_squares(s)
+            if streamed(s - 1):
+                normalise(s - 1)
+            if live(s - 3):
                 rope_add(s - 3)
             if live(s + 1) and s >= 0:
                 carry(s + 1)
-            if s - 1 in items and s - 1 >= first_item:
-                inverse_rms(s - 1)
-            if s == -2:
-                for i in range(10, 12):
-                    turn("w", i, ["z0", "z1"][i - 10])
-                    interleave("w", i, True)
+            if streamed(s):
+                inverse_rms(s)
             if live(s):
                 tap(s, 0)
-            if rotated(s - 2):
+            if live(s - 2):
                 rope_cos(s - 2)
-            if live(s - 2) and not rotated(s - 2):
-                copy_v(s - 2)
-            if s in (0, 1):
-                quantize_w(2, s)
+            if s in (-1, 0):
+                quantize_w(2, s + 1)
+            if s - 1 in late:
+                interleave("x", late[s - 1][0], True)
+            if s in late:
+                turn("x", *late[s])
             if live(s):
                 tap(s, 1)
-            if rotated(s - 2):
-                rope_sin(s - 2)
-            if s == 1:
+            if s == 0:
                 nc.vector.tensor_scalar(out=sin_sb[:, :, 0:D // 2], in0=sin_sb[:, :, 0:D // 2], scalar1=-1.0,
                                         scalar2=None, op0=ALU.mult)
+            if live(s - 2):
+                rope_sin(s - 2)
+            if s - 1 in late and late[s - 1][0] % 2 == 1:
+                quantize_x(late[s - 1][0] - 1, 2)
+            for b, e in v_in(s, 6):
+                v_store(b, e)
             if live(s):
                 tap(s, 2)
-            if s in fill:
-                quantize_x(fill[s], BLOCK_TILES)

@@ -341,7 +341,8 @@ def tile_attention_pa_kernel(tc, x, cos, sin, q_w, k_w, v_w, q_norm_w, k_norm_w,
 
         def v_store(b, e):
             st = work.tile([P, BLOCK_TILES, D], F32, name="stv", tag="stv", bufs=2)
-            nc.vector.tensor_copy(out=st[:], in_=v_bank[b, e][:].rearrange("p (i d) -> p i d", d=D))
+            copy_out = nc.scalar.copy if b == BLOCKS - 1 else nc.vector.tensor_copy
+            copy_out(out=st[:], in_=v_bank[b, e][:].rearrange("p (i d) -> p i d", d=D))
             nc.sync.dma_start(out=out_rows[2][:, BLOCK_TILES * b:BLOCK_TILES * (b + 1), e * D:(e + 1) * D], in_=st[:])
 
         v_phase = {}
@@ -402,7 +403,7 @@ def tile_attention_pa_kernel(tc, x, cos, sin, q_w, k_w, v_w, q_norm_w, k_norm_w,
         def streamed(t):
             return t in items and t >= first_item
 
-        for s in range(first_item, STEPS + 3):
+        for s in range(first_item, STEPS + 4):
             if live(s + 1) and s >= 0:
                 to_channels(s + 1)
             if live(s - 1):
@@ -410,6 +411,19 @@ def tile_attention_pa_kernel(tc, x, cos, sin, q_w, k_w, v_w, q_norm_w, k_norm_w,
                 acts[s - 1] = silu(accs[h][:, 0:BLOCK], h, pivot[:, h:h + 1])
             if streamed(s):
                 project(s)
+            if live(s):
+                tap(s, 0)
+            if live(s - 3):
+                rope_sin(s - 3)
+            if s in (-1, 0):
+                quantize_w(2, s + 1)
+            if s - 1 in late:
+                interleave("x", late[s - 1][0], True)
+            if s in late:
+                turn("x", *late[s])
+            for j in range(TAPS):
+                for b, e in v_in(s, 1 + j):
+                    v_tap(b, e, j)
             if live(s - 1):
                 zs[s - 1] = to_tokens(us[s - 1], acts[s - 1], "z%d" % ((s - 1) % 2))
             if live(s + 1) and s >= 0:
@@ -417,11 +431,6 @@ def tile_attention_pa_kernel(tc, x, cos, sin, q_w, k_w, v_w, q_norm_w, k_norm_w,
             for b, e in v_in(s, 0):
                 v_project(b, e)
                 v_halo(b, e)
-            for b, e in v_in(s, 1):
-                v_copy_u(b, e)
-            for j in range(TAPS):
-                for b, e in v_in(s, 1 + j):
-                    v_tap(b, e, j)
             for b, e in v_in(s, 5):
                 v_act[b, e] = silu(v_bank[b, e][:], V0 + e, 1.0)
                 v_bank[b, e] = to_tokens(v_u[b, e][:, HALO:HALO + BLOCK], v_act[b, e], "v%d" % e)
@@ -429,29 +438,21 @@ def tile_attention_pa_kernel(tc, x, cos, sin, q_w, k_w, v_w, q_norm_w, k_norm_w,
                 sum_squares(s)
             if streamed(s - 1):
                 normalise(s - 1)
-            if live(s - 3):
-                rope_add(s - 3)
+            for b, e in v_in(s, 0):
+                v_copy_u(b, e)
+            if live(s - 4):
+                rope_add(s - 4)
             if live(s + 1) and s >= 0:
                 carry(s + 1)
             if streamed(s):
                 inverse_rms(s)
-            if live(s):
-                tap(s, 0)
-            if live(s - 2):
-                rope_cos(s - 2)
-            if s in (-1, 0):
-                quantize_w(2, s + 1)
-            if s - 1 in late:
-                interleave("x", late[s - 1][0], True)
-            if s in late:
-                turn("x", *late[s])
             if live(s):
                 tap(s, 1)
             if s == 0:
                 nc.vector.tensor_scalar(out=sin_sb[:, :, 0:D // 2], in0=sin_sb[:, :, 0:D // 2], scalar1=-1.0,
                                         scalar2=None, op0=ALU.mult)
             if live(s - 2):
-                rope_sin(s - 2)
+                rope_cos(s - 2)
             if s - 1 in late and late[s - 1][0] % 2 == 1:
                 quantize_x(late[s - 1][0] - 1, 2)
             for b, e in v_in(s, 6):

@@ -77,7 +77,13 @@ def tile_attention_pa_kernel(tc, x, cos, sin, q_w, k_w, v_w, q_norm_w, k_norm_w,
         nc.scalar.dma_start(out=par_raw[0:HEADS, TAPS * D:], in_=canon_bias.rearrange("(h p) -> h p", p=P))
         nc.scalar.dma_start(out=par_raw[HEADS:HEADS + 1, TAPS * D:], in_=q_norm_w.rearrange("(o d) -> o d", o=1))
         nc.scalar.dma_start(out=par_raw[HEADS + 1:HEADS + 2, TAPS * D:], in_=k_norm_w.rearrange("(o d) -> o d", o=1))
+        warm = keep.tile([P, 1], F32)
+        nc.scalar.activation(out=warm[:], in_=ident[:, 0:1], func=ACT.Silu)
         par_rows = keep.tile([P, TAPS + 1, D], F32)
+        ones = keep.tile([P, 1], F32)
+        warm_pow = keep.tile([P, 1], F32)
+        nc.gpsimd.memset(ones[:], 1.0)
+        nc.gpsimd.tensor_tensor(out=warm_pow[:], in0=ones[:], in1=ones[:], op=ALU.pow)
         nc.gpsimd.tensor_copy(out=par_rows[:, 0:TAPS, :], in_=par_raw[:, 0:TAPS * D].rearrange("p (c j) -> p j c", j=TAPS))
         nc.gpsimd.tensor_copy(out=par_rows[:, TAPS, :], in_=par_raw[:, TAPS * D:])
         minus_half = keep.tile([P, 4], F32)

from contextlib import ExitStack

import concourse.mybir as mybir
from concourse.masks import make_identity

S, HID, D = 2048, 1024, 128
Q_HEADS, KV_HEADS = 8, 2
HEADS = Q_HEADS + 2 * KV_HEADS
TAPS = 4
EPS = 1e-5
FLOPS = 2 * S * HID * HEADS * D

F32 = mybir.dt.float32
BF16 = mybir.dt.bfloat16
U32 = mybir.dt.uint32
U8 = mybir.dt.uint8
E4M3 = mybir.dt.float8_e4m3fn_x4
E5M2 = mybir.dt.float8_e5m2_x4
ALU = mybir.AluOpType
ACT = mybir.ActivationFunctionType

P = 128
PASSES = HID // 512
TILES = S // P
BLOCK_TILES = 4
BLOCK = BLOCK_TILES * P
BLOCKS = S // BLOCK
HALO = TAPS - 1
ACC_W = 520
K0 = Q_HEADS
V0 = Q_HEADS + KV_HEADS
STEPS = BLOCKS * V0
LEAD = 6
V_START = (1, 6)
V_START_LAST = (1, 4)
U_BUFS = 4
TINY = 2.0 ** -40


def tile_attention_pa_kernel(tc, x, cos, sin, q_w, k_w, v_w, q_norm_w, k_norm_w,
                                         canon_w, canon_bias, out_0, out_1, out_2):
    nc = tc.nc
    with ExitStack() as ctx:
        keep = ctx.enter_context(tc.tile_pool(name="keep", bufs=1))
        work = ctx.enter_context(tc.tile_pool(name="work", bufs=1))
        psum = ctx.enter_context(tc.psum_pool(name="psum", bufs=1))
        ctx.enter_context(tc.manual_schedule())

        def bank(tag):
            return psum.tile([P, 512], F32, name=tag, tag=tag)

        ident = keep.tile([P, P], F32)
        make_identity(nc, ident[:])

        x_rows = x.rearrange("b (i p) k -> p (b i) k", p=P)
        q_rows = q_w.rearrange("(i p) k -> p i k", p=P)
        w_raw = keep.tile([P, HEADS, HID], BF16)
        x_raw = keep.tile([P, TILES, HID], BF16)
        cos_sb = keep.tile([P, TILES, D], BF16)
        sin_sb = keep.tile([P, TILES, D], BF16)
        nc.sync.dma_start(out=w_raw[:, 0:1, :], in_=q_rows[:, 0:1, :])
        nc.sync.dma_start(out=w_raw[:, 1:4, :], in_=q_rows[:, 1:4, :])
        nc.sync.dma_start(out=x_raw[:, 0:2, :], in_=x_rows[:, 0:2, :])
        nc.sync.dma_start(out=x_raw[:, 2:4, :], in_=x_rows[:, 2:4, :])
        nc.sync.dma_start(out=w_raw[:, 4:8, :], in_=q_rows[:, 4:8, :])
        nc.sync.dma_start(out=w_raw[:, K0:V0, :], in_=k_w.rearrange("(i p) k -> p i k", p=P))
        nc.sync.dma_start(out=w_raw[:, V0:HEADS, :], in_=v_w.rearrange("(i p) k -> p i k", p=P))
        nc.sync.dma_start(out=x_raw[:, 4:8, :], in_=x_rows[:, 4:8, :])
        nc.sync.dma_start(out=cos_sb[:], in_=cos.rearrange("(i p) d -> p i d", p=P))
        nc.sync.dma_start(out=sin_sb[:], in_=sin.rearrange("(i p) d -> p i d", p=P))
        nc.sync.dma_start(out=x_raw[:, 8:12, :], in_=x_rows[:, 8:12, :])
        nc.sync.dma_start(out=x_raw[:, 12:16, :], in_=x_rows[:, 12:16, :])

        par_raw = keep.tile([P, (TAPS + 1) * D], BF16)
        nc.gpsimd.memset(par_raw[:], 0.0)
        nc.scalar.dma_start(out=par_raw[0:HEADS, 0:TAPS * D], in_=canon_w.rearrange("(h p) j -> h (p j)", p=P))
        nc.scalar.dma_start(out=par_raw[0:HEADS, TAPS * D:], in_=canon_bias.rearrange("(h p) -> h p", p=P))
        nc.scalar.dma_start(out=par_raw[HEADS:HEADS + 1, TAPS * D:], in_=q_norm_w.rearrange("(o d) -> o d", o=1))
        nc.scalar.dma_start(out=par_raw[HEADS + 1:HEADS + 2, TAPS * D:], in_=k_norm_w.rearrange("(o d) -> o d", o=1))
        warm = keep.tile([P, 1], F32)
        nc.scalar.activation(out=warm[:], in_=ident[:, 0:1], func=ACT.Silu)
        par_rows = keep.tile([P, TAPS + 1, D], F32)
        ones = keep.tile([P, 1], F32)
        warm_pow = keep.tile([P, 1], F32)
        nc.gpsimd.memset(ones[:], 1.0)
        nc.gpsimd.tensor_tensor(out=warm_pow[:], in0=ones[:], in1=ones[:], op=ALU.pow)
        nc.gpsimd.tensor_copy(out=par_rows[:, 0:TAPS, :], in_=par_raw[:, 0:TAPS * D].rearrange("p (c j) -> p j c", j=TAPS))
        nc.gpsimd.tensor_copy(out=par_rows[:, TAPS, :], in_=par_raw[:, TAPS * D:])
        minus_half = keep.tile([P, 4], F32)
        nc.gpsimd.memset(minus_half[:], -0.5)
        par = keep.tile([P, TAPS + 1, 16], F32)
        tap_n = keep.tile([P, HALO, V0], F32)
        pivot = keep.tile([P, V0], F32)
        small = keep.tile([P, V0], F32)
        inverse = keep.tile([P, V0], F32)

        def constants(tag_a, tag_b):
            a = bank(tag_a)
            b = bank(tag_b)
            for j in range(TAPS):
                nc.tensor.transpose(a[:, j * D:(j + 1) * D], par_rows[:, j, :], ident[:])
            nc.tensor.transpose(b[:, 0:D], par_rows[:, TAPS, :], ident[:])
            nc.vector.tensor_copy(out=par[:, 0:TAPS, :], in_=a[:].rearrange("p (j c) -> p j c", j=TAPS)[:, :, 0:16])
            nc.vector.tensor_copy(out=par[:, TAPS, :], in_=b[:, 0:16])

        diag = keep.tile([P, KV_HEADS, TAPS, P], F32)

        def tap_diagonals():
            for e in range(KV_HEADS):
                for j in range(TAPS):
                    nc.vector.tensor_scalar(out=diag[:, e, j, :], in0=ident[:], scalar1=par[:, j, V0 + e:V0 + e + 1],
                                            scalar2=None, op0=ALU.mult)

        def fold_norm_weights():
            last = par[:, HALO, 0:V0]
            nc.vector.tensor_tensor(out=small[:], in0=last, in1=last, op=ALU.mult)
            nc.vector.tensor_scalar(out=small[:], in0=small[:], scalar1=TINY * TINY, scalar2=2.0 * TINY,
                                    op0=ALU.is_lt, op1=ALU.mult)
            nc.vector.tensor_tensor(out=pivot[:], in0=last, in1=small[:], op=ALU.add)
            nc.vector.reciprocal(out=inverse[:], in_=pivot[:])
            nc.vector.tensor_tensor(out=tap_n[:], in0=par[:, 0:HALO, 0:V0],
                                    in1=inverse[:].unsqueeze(1).to_broadcast([P, HALO, V0]), op=ALU.mult)
            nc.vector.tensor_scalar(out=tap_n[:, :, 0:K0], in0=tap_n[:, :, 0:K0],
                                    scalar1=par[:, TAPS, HEADS:HEADS + 1], scalar2=None, op0=ALU.mult)
            nc.vector.tensor_scalar(out=tap_n[:, :, K0:V0], in0=tap_n[:, :, K0:V0],
                                    scalar1=par[:, TAPS, HEADS + 1:HEADS + 2], scalar2=None, op0=ALU.mult)

        x_codes = keep.tile([P, TILES, PASSES, P], U32, align_bytes=64)
        x_scales = keep.tile([P, TILES, PASSES, P], U8, align_bytes=64)
        w_codes = keep.tile([P, 3, PASSES, 512], U32, align_bytes=64)
        w_scales = keep.tile([P, 3, PASSES, 512], U8, align_bytes=64)
        turned = {}
        grouped = {}

        def turn(kind, i, tag):
            raw = x_raw if kind == "x" else w_raw
            words = raw[:, i, :].bitcast(F32)
            t = bank(tag)
            for g in range(PASSES):
                for u in range(2):
                    c = (2 * g + u) * P
                    nc.tensor.transpose(t[:, c:c + P], words[:, 256 * g + u:256 * (g + 1):2], ident[:])
            turned[kind, i] = t

        def interleave(kind, i, on_vector):
            src = turned[kind, i][:].rearrange("p (g u r) -> p g r u", g=PASSES, u=2)
            if kind == "x":
                if i % 4 == 0:
                    grouped[kind, i // 4] = work.tile([P, BLOCK_TILES, HID], BF16, name="xg", tag="xg", bufs=1, align_bytes=64)
                dst = grouped[kind, i // 4][:, i % 4, :].bitcast(F32).rearrange("p (g r u) -> p g r u", g=PASSES, u=2)
            else:
                if i % 4 == 0:
                    grouped[kind, i // 4] = work.tile([P, PASSES, 2048], BF16, name="wg", tag="wg", bufs=1, align_bytes=64)
                r0 = 256 * (i % 4)
                dst = grouped[kind, i // 4][:].bitcast(F32)[:, :, r0:r0 + 256].rearrange("p g (r u) -> p g r u", u=2)
            if on_vector:
                nc.vector.tensor_copy(out=dst, in_=src)
            else:
                nc.scalar.copy(out=dst, in_=src)

        def quantize_x(i, count):
            nc.vector.quantize_mx(
                out=x_codes[:, i:i + count, :, :].rearrange("p i g r -> p (i g r)").bitcast(E5M2),
                scales=x_scales[:, i:i + count, :, :].rearrange("p i g r -> p (i g r)"),
                in_=grouped["x", i // 4][:, i % 4:i % 4 + count, :].rearrange("p i k -> p (i k)"))

        def quantize_w(grp, g):
            nc.vector.quantize_mx(out=w_codes[:, grp, g, :].bitcast(E4M3), scales=w_scales[:, grp, g, :],
                                  in_=grouped["w", grp][:, g, :])

        items = {}
        for b in range(BLOCKS):
            for n in range(10):
                items[V0 * b - LEAD + n] = (b, n)
        proj = {}
        sums = {}
        rstd = {}
        normed = {}

        def project(t, tag=None):
            b, n = items[t]
            acc = bank(tag or "m%d" % (t % 2))
            if n < 8:
                parts = [(BLOCK_TILES * b + n % 4, n // 4, 0, 512)]
            else:
                parts = [(BLOCK_TILES * b + 2 * (n - 8) + e, 2, 256 * e, 256) for e in range(2)]
            for i, grp, c0, width in parts:
                for g in range(PASSES):
                    nc.tensor.matmul_mx(
                        out=acc[:, c0:c0 + width],
                        lhsT=x_codes[:, i, g, :].bitcast(E5M2), lhsT_scale=x_scales[:, i, g, :],
                        rhs=w_codes[:, grp, g, 0:width].bitcast(E4M3), rhs_scale=w_scales[:, grp, g, 0:width],
                        start=(g == 0), stop=(g == PASSES - 1))
            proj[t] = acc

        def sum_squares(t):
            ss = work.tile([P, 4], F32, name="ss", tag="ss", bufs=3)
            squares = work.tile([P, 4, D], BF16, name="squares", tag="squares", bufs=2)
            for e in range(4):
                nc.scalar.activation(out=squares[:, e, :], in_=proj[t][:, e * D:(e + 1) * D], func=ACT.Square,
                                     accum_out=ss[:, e:e + 1])
            ms = work.tile([P, 4], F32, name="ms", tag="ms", bufs=3)
            nc.scalar.activation(out=ms[:], in_=ss[:], func=ACT.Copy, scale=1.0 / D, bias=EPS)
            sums[t] = ms

        def inverse_rms(t):
            r = work.tile([P, 4], F32, name="r", tag="r", bufs=4)
            nc.gpsimd.tensor_tensor(out=r[:], in0=sums[t][:], in1=minus_half[:], op=ALU.pow)
            rstd[t] = r

        def normalise(t):
            b, n = items[t]
            grp = n // 4
            if n % 4 == 0:
                normed[b, grp] = work.tile([P, BLOCK_TILES, 512], F32, name="nb", tag="nb", bufs=3)
            for e in range(4):
                if n < 8:
                    dst = normed[b, grp][:, n % 4, e * D:(e + 1) * D]
                else:
                    dst = normed[b, grp][:, 2 * (n - 8) + e // 2, (e % 2) * D:(e % 2 + 1) * D]
                nc.scalar.activation(out=dst, in_=proj[t][:, e * D:(e + 1) * D], func=ACT.Copy,
                                     scale=rstd[t][:, e:e + 1])

        acc_all = keep.tile([P, V0, ACC_W], F32)
        nc.gpsimd.memset(acc_all[:, :, BLOCK:BLOCK + HALO], 0.0)
        u_all = keep.tile([P, U_BUFS, ACC_W], F32)
        nc.gpsimd.memset(u_all[:, :, BLOCK:BLOCK + HALO], 0.0)
        accs = [acc_all[:, h, :] for h in range(V0)]
        chan = {}
        us = {}
        acts = {}
        zs = {}
        rot = {}
        stage = {}
        out_rows = [o.rearrange("b (i p) h d -> p (b i) (h d)", p=P) for o in (out_0, out_1, out_2)]

        def to_channels(s):
            b, h = divmod(s, V0)
            t = bank("n%d" % (s % 2))
            for i in range(BLOCK_TILES):
                nc.tensor.transpose(t[:, i * P:(i + 1) * P], normed[b, h // 4][:, i, (h % 4) * D:(h % 4 + 1) * D], ident[:])
            chan[s] = t

        def copy_u(s):
            h = s % V0
            u = u_all[:, s % U_BUFS, :]
            col = HEADS if h < K0 else HEADS + 1
            nc.scalar.activation(out=u[:, 0:BLOCK], in_=chan[s][:], func=ACT.Copy, scale=par[:, TAPS, col:col + 1])
            us[s] = u

        def carry(s):
            h = s % V0
            nc.gpsimd.tensor_tensor(out=accs[h][:, 0:HALO], in0=accs[h][:, BLOCK:BLOCK + HALO], in1=us[s][:, 0:HALO],
                                    op=ALU.add)

        def tap(s, j):
            h = s % V0
            shift = HALO - j
            w = BLOCK
            onto = us[s] if j == 0 else accs[h]
            nc.vector.scalar_tensor_tensor(out=accs[h][:, shift:shift + w], in0=chan[s][:, 0:w], scalar=tap_n[:, j, h:h + 1],
                                           in1=onto[:, shift:shift + w], op0=ALU.mult, op1=ALU.add)

        def silu(pre, h, scale):
            a = work.tile([P, BLOCK], F32, name="a", tag="a", bufs=4)
            nc.scalar.activation(out=a[:], in_=pre, func=ACT.Silu, scale=scale, bias=par[:, TAPS, h:h + 1])
            return a

        def to_tokens(u, a, tag):
            z = bank(tag)
            for i in range(BLOCK_TILES):
                cols = slice(i * P, (i + 1) * P)
                nc.tensor.matmul(z[:, cols], lhsT=u[:, cols], rhs=ident[:], is_transpose=True, start=True, stop=False)
                nc.tensor.matmul(z[:, cols], lhsT=a[:, cols], rhs=ident[:], is_transpose=True, start=False, stop=True)
            return z

        def unit(s):
            b, h = divmod(s, V0)
            return b, h, h - h % 4, 4 if h < K0 else KV_HEADS

        def staged(s):
            b, h, first, count = unit(s)
            if (b, first) not in stage:
                stage[b, first] = work.tile([P, BLOCK_TILES, count * D], F32, name="st", tag="st", bufs=3)
            return stage[b, first][:, :, (h - first) * D:(h - first + 1) * D]

        def rope_cos(s):
            b = s // V0
            nc.vector.tensor_tensor(out=staged(s), in0=zs[s][:].rearrange("p (i d) -> p i d", d=D),
                                    in1=cos_sb[:, BLOCK_TILES * b:BLOCK_TILES * (b + 1), :], op=ALU.mult)

        def rope_sin(s):
            b = s // V0
            t = work.tile([P, BLOCK_TILES, D], F32, name="rot", tag="rot", bufs=3)
            swapped = zs[s][:].rearrange("p (i e d) -> p i e d", e=2, d=D // 2)[:, :, ::-1, :]
            nc.vector.tensor_tensor(
                out=t[:].rearrange("p i (e d) -> p i e d", e=2), in0=swapped,
                in1=sin_sb[:, BLOCK_TILES * b:BLOCK_TILES * (b + 1), :].rearrange("p i (e d) -> p i e d", e=2),
                op=ALU.mult)
            rot[s] = t

        def rope_add(s):
            engine = nc.vector if s == STEPS - 1 else nc.gpsimd
            engine.tensor_tensor(out=staged(s), in0=staged(s), in1=rot[s][:], op=ALU.add)
            b, h, first, count = unit(s)
            tiles = slice(BLOCK_TILES * b, BLOCK_TILES * (b + 1))
            if s >= STEPS - KV_HEADS:
                e = h - first
                nc.sync.dma_start(out=out_rows[1][:, tiles, e * D:(e + 1) * D], in_=staged(s))
            elif h == first + count - 1:
                which, c0 = (0, first * D) if h < K0 else (1, 0)
                nc.sync.dma_start(out=out_rows[which][:, tiles, c0:c0 + count * D], in_=stage[b, first][:])

        v_bank = {}
        v_u = {}
        v_act = {}

        def v_project(b, e):
            t = bank("v%d" % e)
            c0 = (KV_HEADS + e) * D
            for i in range(BLOCK_TILES):
                for g in range(PASSES):
                    nc.tensor.matmul_mx(
                        out=t[:, i * P:(i + 1) * P],
                        lhsT=w_codes[:, 2, g, c0:c0 + D].bitcast(E4M3), lhsT_scale=w_scales[:, 2, g, c0:c0 + D],
                        rhs=x_codes[:, BLOCK_TILES * b + i, g, :].bitcast(E5M2),
                        rhs_scale=x_scales[:, BLOCK_TILES * b + i, g, :],
                        start=(g == 0), stop=(g == PASSES - 1))
            v_bank[b, e] = t

        def v_halo(b, e):
            u = work.tile([P, ACC_W], F32, name="uv", tag="uv", bufs=3)
            if b == 0:
                nc.gpsimd.memset(u[:, 0:HALO], 0.0)
            else:
                nc.gpsimd.tensor_copy(out=u[:, 0:HALO], in_=v_u[b - 1, e][:, BLOCK:BLOCK + HALO])
            v_u[b, e] = u

        def v_copy_u(b, e):
            nc.scalar.copy(out=v_u[b, e][:, HALO:HALO + BLOCK], in_=v_bank[b, e][:])

        def v_tap(b, e, j):
            if j == 0:
                v_bank[b, e] = bank("v%d" % e)
            nc.tensor.matmul(v_bank[b, e][:], lhsT=diag[:, e, j, :], rhs=v_u[b, e][:, j:j + BLOCK],
                             start=(j == 0), stop=(j == TAPS - 1))

        def v_store(b, e):
            st = work.tile([P, BLOCK_TILES, D], F32, name="stv", tag="stv", bufs=2)
            copy_out = nc.scalar.copy if b == BLOCKS - 1 else nc.vector.tensor_copy
            copy_out(out=st[:], in_=v_bank[b, e][:].rearrange("p (i d) -> p i d", d=D))
            nc.sync.dma_start(out=out_rows[2][:, BLOCK_TILES * b:BLOCK_TILES * (b + 1), e * D:(e + 1) * D], in_=st[:])

        v_phase = {}
        late = {}
        for b in range(BLOCKS):
            for e in range(KV_HEADS):
                for phase in range(7):
                    v_phase.setdefault(V0 * b + (V_START if b < BLOCKS - 1 else V_START_LAST)[e] + phase, []).append((b, e, phase))
        for b in range(1, BLOCKS):
            for i in range(BLOCK_TILES):
                late[V0 * (b - 1) + (-2, -1, 3, 4)[i]] = (BLOCK_TILES * b + i, "v%d" % (i // 2))

        def v_in(s, phase):
            return [(b, e) for b, e, p in v_phase.get(s, []) if p == phase]

        def live(s):
            return 0 <= s < STEPS

        for i in range(4):
            turn("w", i, ["n0", "n1", "z0", "z1"][i])
            interleave("w", i, i % 2 == 0)
        for i in range(4):
            turn("x", i, ["v0", "v1", "n0", "n1"][i])
        quantize_w(0, 0)
        interleave("x", 0, False)
        quantize_w(0, 1)
        interleave("x", 1, False)
        quantize_x(0, 1)
        interleave("x", 2, True)
        quantize_x(1, 1)
        interleave("x", 3, False)
        quantize_x(2, 1)
        quantize_x(3, 1)
        constants("z0", "z1")
        fold_norm_weights()
        tap_diagonals()
        for n in range(4):
            project(n - LEAD, ["m0", "m1", "v0", "v1"][n])
            sum_squares(n - LEAD)
            inverse_rms(n - LEAD)
        for i in range(4, 8):
            turn("w", i, ["n0", "n1", "z0", "z1"][i - 4])
            interleave("w", i, True)
        quantize_w(1, 0)
        quantize_w(1, 1)
        for n in range(4):
            normalise(n - LEAD)
        for i in range(8, 11):
            turn("w", i, ["n1", "z0", "z1"][i - 8])
            interleave("w", i, True)
        to_channels(0)
        copy_u(0)
        carry(0)
        turn("w", 11, "v1")
        interleave("w", 11, False)
        first_item = 4 - LEAD

        def streamed(t):
            return t in items and t >= first_item

        for s in range(first_item, STEPS + 4):
            if live(s + 1) and s >= 0:
                to_channels(s + 1)
            if live(s - 1):
                h = (s - 1) % V0
                acts[s - 1] = silu(accs[h][:, 0:BLOCK], h, pivot[:, h:h + 1])
            if streamed(s):
                project(s)
            if live(s):
                tap(s, 0)
            if live(s - 3):
                rope_sin(s - 3)
            if s in (-1, 0):
                quantize_w(2, s + 1)
            if s - 1 in late:
                interleave("x", late[s - 1][0], True)
            if s in late:
                turn("x", *late[s])
            for j in range(TAPS):
                for b, e in v_in(s, 1 + j):
                    v_tap(b, e, j)
            if live(s - 1):
                zs[s - 1] = to_tokens(us[s - 1], acts[s - 1], "z%d" % ((s - 1) % 2))
            if live(s + 1) and s >= 0:
                copy_u(s + 1)
            for b, e in v_in(s, 0):
                v_project(b, e)
                v_halo(b, e)
            for b, e in v_in(s, 5):
                v_act[b, e] = silu(v_bank[b, e][:], V0 + e, 1.0)
                v_bank[b, e] = to_tokens(v_u[b, e][:, HALO:HALO + BLOCK], v_act[b, e], "v%d" % e)
            if streamed(s):
                sum_squares(s)
            if streamed(s - 1):
                normalise(s - 1)
            for b, e in v_in(s, 0):
                v_copy_u(b, e)
            if live(s - 4):
                rope_add(s - 4)
            if live(s + 1) and s >= 0:
                carry(s + 1)
            if streamed(s):
                inverse_rms(s)
            if live(s):
                tap(s, 1)
            if s == 0:
                nc.vector.tensor_scalar(out=sin_sb[:, :, 0:D // 2], in0=sin_sb[:, :, 0:D // 2], scalar1=-1.0,
                                        scalar2=None, op0=ALU.mult)
            if live(s - 2):
                rope_cos(s - 2)
            if s - 1 in late and late[s - 1][0] % 2 == 1:
                quantize_x(late[s - 1][0] - 1, 2)
            for b, e in v_in(s, 6):
                v_store(b, e)
            if live(s):
                tap(s, 2)
